import numpy as np
import ml_dtypes


def mxq(x, axis, fmt="e4m3"):
    dtype, down = {"e4m3": (ml_dtypes.float8_e4m3fn, 7), "e5m2": (ml_dtypes.float8_e5m2, 14)}[fmt]
    v = np.moveaxis(np.asarray(x, np.float32).astype(ml_dtypes.bfloat16).astype(np.float64), axis, -1)
    blocks = v.reshape(v.shape[:-1] + (-1, 32))
    amax = np.abs(blocks).max(-1, keepdims=True)
    byte = np.maximum(np.where(amax > 0, np.frexp(amax)[1] - 1 + 127, 0) - down, 1)
    scale = np.exp2(byte - 127.0)
    codes = (blocks / scale).astype(np.float32).astype(dtype).astype(np.float64)
    return np.moveaxis((codes * scale).reshape(v.shape), -1, axis)


WIDE = False


def mx_kscale(k):
    if not WIDE:
        return np.ones(k)
    levels = np.array([10, -10, 5, -5, 0])
    a = np.random.permutation(np.resize(levels, k // 512 * 4)).reshape(k // 512, 4)
    idx = np.arange(k)
    return np.exp2(a[idx // 512, idx % 128 // 32])


BF16 = ml_dtypes.bfloat16


def bf(x):
    return np.asarray(x, np.float32).astype(BF16)


def f64(x):
    return np.asarray(x).astype(np.float64)


BS, NB, BD, H = 4096, 2, 512, 512
D = NB * BD
G = BS * NB // BD
ZMAX, NTERMS = 6.0, 120


def erf(z):
    a = np.minimum(np.abs(z), ZMAX)
    q = a * a
    term = a.copy()
    tot = a.copy()
    for n in range(1, NTERMS):
        term = term * q / (n + 0.5)
        tot = tot + term
    return np.sign(z) * np.minimum(tot * np.exp(-q) / (0.5 * np.sqrt(np.pi)), 1.0)


def gelu(v):
    return 0.5 * v * (1.0 + erf(v * np.sqrt(0.5)))


def setup_inputs():
    s = mx_kscale(BD)
    y = np.random.standard_normal((G, BD, BD)) * s[None, :, None]
    return {"y0": bf(y.reshape(BS, D)),
            "W1": bf(np.random.standard_normal((NB, BD, H)) / np.sqrt(BD) / s[None, :, None]),
            "b1": bf(np.random.standard_normal((NB, 1, H)) * 0.2),
            "W2": bf(np.random.standard_normal((NB, H, BD)) * 1.5 / np.sqrt(H)),
            "b2": bf(np.random.standard_normal((NB, 1, BD)) * 0.2)}


def reference(y0, W1, b1, W2, b2):
    z = f64(y0).reshape(-1, BD, BD).transpose(0, 2, 1).reshape(BS, -1)
    zb = z.reshape(BS, NB, BD).transpose(1, 0, 2)
    h = gelu((mxq(zb, 2, "e4m3") @ mxq(f64(W1), 1, "e4m3")) + f64(b1))
    o = (mxq(h, 2, "e4m3") @ mxq(f64(W2), 1, "e4m3")) + f64(b2)
    o = o.transpose(1, 0, 2).reshape(BS, -1)
    return o.reshape(-1, BD, BD).transpose(0, 2, 1).reshape(BS, -1)

@@ -1,0 +1,203 @@
+from contextlib import ExitStack
+
+import concourse.mybir as mybir
+
+BF16 = mybir.dt.bfloat16
+F32 = mybir.dt.float32
+U32 = mybir.dt.uint32
+U8 = mybir.dt.uint8
+FP8X4 = mybir.dt.float8_e4m3fn_x4
+GELU = mybir.ActivationFunctionType.Gelu
+ADD = mybir.AluOpType.add
+
+P = 128
+PACK = 4
+WIDTH = P * PACK
+BLOCKS = 2
+GROUPS = 16
+GROUP_TOKENS = WIDTH // BLOCKS
+UNIT_GROUPS = 2
+UNIT_TOKENS = UNIT_GROUPS * GROUP_TOKENS
+UNITS = GROUPS * BLOCKS // UNIT_GROUPS
+FLOPS = 2 * 2 * GROUPS * WIDTH * WIDTH * WIDTH
+
+
+def tile_blockmlp_mixerblock_pa_t_kernel(tc, y0, W1, b1, W2, b2, out):
+    nc = tc.nc
+    y_pairs = y0.rearrange("(q g p r) w -> q p g (r w)", g=UNIT_GROUPS, p=P, r=2)
+    out_groups = out.rearrange("(g p r) w -> g p (r w)", p=P, r=2)
+
+    with ExitStack() as stack:
+        keep = stack.enter_context(tc.tile_pool(name="keep", bufs=1))
+        stage = stack.enter_context(tc.tile_pool(name="stage", bufs=2))
+        hidden_banks = stack.enter_context(tc.psum_pool(name="hidden_banks", bufs=4))
+        out_banks = stack.enter_context(tc.psum_pool(name="out_banks", bufs=4))
+        stack.enter_context(tc.manual_schedule())
+
+        b1_raw = keep.tile([P, BLOCKS, PACK], BF16)
+        b2_raw = keep.tile([P, BLOCKS, PACK], BF16)
+        nc.scalar.dma_start(out=b1_raw[:], in_=b1.rearrange("n o (m t) -> m (n o) t", t=PACK))
+        nc.scalar.dma_start(out=b2_raw[:], in_=b2.rearrange("n o (m t) -> m (n o) t", t=PACK))
+
+        w_raw = {}
+        y_raw = {}
+
+        def load_weights(layer, w, block):
+            raw = keep.tile([P, PACK, WIDTH], BF16, name="w_raw%d%d" % (layer, block))
+            nc.sync.dma_start(out=raw[:], in_=w[block].rearrange("(p j) h -> p j h", j=PACK))
+            w_raw[(layer, block)] = raw
+
+        def load_pair(pair):
+            raw = keep.tile([P, UNIT_GROUPS, PACK * WIDTH], BF16, name="y_raw%d" % pair)
+            nc.sync.dma_start(out=raw[:], in_=y_pairs[pair])
+            y_raw[pair] = raw
+
+        load_weights(1, W1, 0)
+        load_pair(0)
+        load_weights(1, W1, 1)
+        load_pair(1)
+        load_weights(2, W2, 0)
+        load_weights(2, W2, 1)
+        for pair in range(2, GROUPS // UNIT_GROUPS):
+            load_pair(pair)
+
+        warm = keep.tile([P, 1], F32)
+        nc.vector.memset(warm[:], 0.0)
+        nc.scalar.activation(out=warm[:], in_=warm[:], func=GELU)
+
+        b1f = keep.tile([P, BLOCKS, PACK], F32)
+        b2f = keep.tile([P, PACK, BLOCKS], F32)
+        nc.vector.tensor_copy(out=b1f[:], in_=b1_raw[:])
+        nc.vector.tensor_copy(out=b2f[:], in_=b2_raw[:].rearrange("p n s -> p s n"))
+
+        w_codes = {}
+        w_scales = {}
+        for layer in (1, 2):
+            w_codes[layer] = keep.tile([P, BLOCKS, WIDTH], U32, name="w_codes%d" % layer, align_bytes=64)
+            w_scales[layer] = keep.tile([P, BLOCKS, WIDTH], U8, name="w_scales%d" % layer, align_bytes=64)
+
+        def prepare_weights(layer, block):
+            w_grouped = stage.tile([P, PACK, P, PACK], BF16, align_bytes=64)
+            nc.vector.tensor_copy(
+                out=w_grouped[:], in_=w_raw[(layer, block)][:].rearrange("p j (m t) -> p t m j", t=PACK)
+            )
+            nc.vector.quantize_mx(
+                out=w_codes[layer][:, block, :].bitcast(FP8X4),
+                scales=w_scales[layer][:, block, :],
+                in_=w_grouped[:].rearrange("p t m j -> p (t m j)"),
+            )
+
+        z_grouped_of = {}
+        z_packed_of = {}
+        hidden_banks_of = {}
+        h_planes_of = {}
+        h_grouped_of = {}
+        h_packed_of = {}
+        out_banks_of = {}
+
+        def regroup_z(unit, copy):
+            pair, block = divmod(unit, BLOCKS)
+            z_grouped = stage.tile([P, UNIT_TOKENS, PACK], BF16, align_bytes=64, bufs=3)
+            copy(
+                out=z_grouped[:].rearrange("p (g c) j -> p g c j", g=UNIT_GROUPS),
+                in_=y_raw[pair][:].rearrange("p g (j c n) -> p n g c j", j=PACK, n=BLOCKS)[:, block],
+            )
+            z_grouped_of[unit] = z_grouped
+
+        def quantise(grouped, name, bufs):
+            codes = stage.tile([P, UNIT_TOKENS], U32, align_bytes=64, name=name + "_codes", bufs=bufs)
+            scales = stage.tile([P, UNIT_TOKENS], U8, align_bytes=64, name=name + "_scales", bufs=bufs)
+            nc.vector.quantize_mx(
+                out=codes[:].bitcast(FP8X4), scales=scales[:], in_=grouped[:].rearrange("p c j -> p (c j)")
+            )
+            return codes, scales
+
+        def layer1_pass(unit, t):
+            block = unit % BLOCKS
+            codes, scales = z_packed_of[unit]
+            bank = hidden_banks.tile([P, UNIT_TOKENS], F32)
+            nc.tensor.matmul_mx(
+                out=bank[:],
+                lhsT=w_codes[1][:, block, t * P : (t + 1) * P].bitcast(FP8X4),
+                lhsT_scale=w_scales[1][:, block, t * P : (t + 1) * P],
+                rhs=codes[:].bitcast(FP8X4),
+                rhs_scale=scales[:],
+                start=True,
+                stop=True,
+            )
+            hidden_banks_of[(unit, t)] = bank
+
+        def gelu(unit):
+            block = unit % BLOCKS
+            h_planes = stage.tile([P, PACK, UNIT_TOKENS], BF16)
+            for t in range(PACK):
+                nc.scalar.activation(
+                    out=h_planes[:, t, :],
+                    in_=hidden_banks_of[(unit, t)][:],
+                    func=GELU,
+                    bias=b1f[:, block, t : t + 1],
+                    scale=1.0,
+                )
+            h_planes_of[unit] = h_planes
+
+        def regroup_h(unit):
+            h_grouped = stage.tile([P, UNIT_TOKENS, PACK], BF16, align_bytes=64)
+            nc.vector.tensor_copy(out=h_grouped[:], in_=h_planes_of[unit][:].rearrange("p t c -> p c t"))
+            h_grouped_of[unit] = h_grouped
+
+        def layer2_passes(group, s):
+            pair, half = divmod(group, UNIT_GROUPS)
+            tokens = slice(half * GROUP_TOKENS, (half + 1) * GROUP_TOKENS)
+            bank = out_banks.tile([P, BLOCKS, GROUP_TOKENS], F32)
+            for block in range(BLOCKS):
+                codes, scales = h_packed_of[pair * BLOCKS + block]
+                nc.tensor.matmul_mx(
+                    out=bank[:, block, :],
+                    lhsT=w_codes[2][:, block, s * P : (s + 1) * P].bitcast(FP8X4),
+                    lhsT_scale=w_scales[2][:, block, s * P : (s + 1) * P],
+                    rhs=codes[:, tokens].bitcast(FP8X4),
+                    rhs_scale=scales[:, tokens],
+                    start=True,
+                    stop=True,
+                )
+            out_banks_of[(group, s)] = bank
+
+        def finish_group(group):
+            rows = stage.tile([P, PACK, WIDTH], F32, bufs=3)
+            for s in range(PACK):
+                nc.vector.tensor_tensor(
+                    out=rows[:, s, :].rearrange("p (c n) -> p c n", n=BLOCKS),
+                    in0=out_banks_of[(group, s)][:].rearrange("p n c -> p c n"),
+                    in1=b2f[:, s, :].unsqueeze(1).to_broadcast([P, GROUP_TOKENS, BLOCKS]),
+                    op=ADD,
+                )
+            nc.sync.dma_start(out=out_groups[group], in_=rows[:].rearrange("p s c -> p (s c)"))
+
+        later_weights = [(1, 1), (2, 0), (2, 1)]
+        prepare_weights(1, 0)
+        regroup_z(0, nc.vector.tensor_copy)
+        regroup_z(1, nc.scalar.copy)
+        z_packed_of[0] = quantise(z_grouped_of[0], "z", 3)
+        for t in range(PACK):
+            layer1_pass(0, t)
+
+        for step in range(UNITS + 3):
+            if step + 1 < UNITS:
+                z_packed_of[step + 1] = quantise(z_grouped_of[step + 1], "z", 3)
+            if step < len(later_weights):
+                prepare_weights(later_weights[step][0], later_weights[step][1])
+            if 0 <= step - 1 < UNITS:
+                h_packed_of[step - 1] = quantise(h_grouped_of[step - 1], "h", 4)
+            if 0 <= step - 3 < GROUPS:
+                finish_group(step - 3)
+            if step < UNITS:
+                gelu(step)
+            for i in range(PACK):
+                if step + 1 < UNITS:
+                    layer1_pass(step + 1, i)
+                if 0 <= step - 2 < GROUPS:
+                    layer2_passes(step - 2, i)
+            if step < UNITS:
+                regroup_h(step)
+            if step + 2 < UNITS:
+                regroup_z(step + 2, nc.scalar.copy)

@@ -129,7 +129,7 @@ def tile_blockmlp_mixerblock_pa_t_kernel(tc, y0, W1, b1, W2, b2, out):
 
         def gelu(unit):
             block = unit % BLOCKS
-            h_planes = stage.tile([P, PACK, UNIT_TOKENS], BF16)
+            h_planes = stage.tile([P, PACK, UNIT_TOKENS], BF16, bufs=3)
             for t in range(PACK):
                 nc.scalar.activation(
                     out=h_planes[:, t, :],
@@ -140,9 +140,9 @@ def tile_blockmlp_mixerblock_pa_t_kernel(tc, y0, W1, b1, W2, b2, out):
                 )
             h_planes_of[unit] = h_planes
 
-        def regroup_h(unit):
+        def regroup_h(unit, copy):
             h_grouped = stage.tile([P, UNIT_TOKENS, PACK], BF16, align_bytes=64)
-            nc.vector.tensor_copy(out=h_grouped[:], in_=h_planes_of[unit][:].rearrange("p t c -> p c t"))
+            copy(out=h_grouped[:], in_=h_planes_of[unit][:].rearrange("p t c -> p c t"))
             h_grouped_of[unit] = h_grouped
 
         def layer2_passes(group, s):
@@ -171,7 +171,7 @@ def tile_blockmlp_mixerblock_pa_t_kernel(tc, y0, W1, b1, W2, b2, out):
                     in1=b2f[:, s, :].unsqueeze(1).to_broadcast([P, GROUP_TOKENS, BLOCKS]),
                     op=ADD,
                 )
-            nc.sync.dma_start(out=out_groups[group], in_=rows[:].rearrange("p s c -> p (s c)"))
+                nc.sync.dma_start(out=out_groups[group][:, s * WIDTH : (s + 1) * WIDTH], in_=rows[:, s, :])
 
         later_weights = [(1, 1), (2, 0), (2, 1)]
         prepare_weights(1, 0)
@@ -181,23 +181,24 @@ def tile_blockmlp_mixerblock_pa_t_kernel(tc, y0, W1, b1, W2, b2, out):
         for t in range(PACK):
             layer1_pass(0, t)
 
-        for step in range(UNITS + 3):
+        for step in range(UNITS + 2):
             if step + 1 < UNITS:
                 z_packed_of[step + 1] = quantise(z_grouped_of[step + 1], "z", 3)
             if step < len(later_weights):
                 prepare_weights(later_weights[step][0], later_weights[step][1])
             if 0 <= step - 1 < UNITS:
                 h_packed_of[step - 1] = quantise(h_grouped_of[step - 1], "h", 4)
-            if 0 <= step - 3 < GROUPS:
-                finish_group(step - 3)
             if step < UNITS:
                 gelu(step)
-            for i in range(PACK):
-                if step + 1 < UNITS:
-                    layer1_pass(step + 1, i)
-                if 0 <= step - 2 < GROUPS:
-                    layer2_passes(step - 2, i)
-            if step < UNITS:
-                regroup_h(step)
-            if step + 2 < UNITS:
-                regroup_z(step + 2, nc.scalar.copy)
+                if step + 2 < UNITS:
+                    regroup_h(step, nc.vector.tensor_copy)
+                    regroup_z(step + 2, nc.scalar.copy)
+                else:
+                    regroup_h(step, nc.scalar.copy)
+            if step + 1 < UNITS:
+                for t in range(PACK):
+                    layer1_pass(step + 1, t)
+            if 0 <= step - 2 < GROUPS:
+                for s in range(PACK):
+                    layer2_passes(step - 2, s)
+                finish_group(step - 2)

@@ -19,6 +19,7 @@ GROUP_TOKENS = WIDTH // BLOCKS
 UNIT_GROUPS = 2
 UNIT_TOKENS = UNIT_GROUPS * GROUP_TOKENS
 UNITS = GROUPS * BLOCKS // UNIT_GROUPS
+RUN = 4
 FLOPS = 2 * 2 * GROUPS * WIDTH * WIDTH * WIDTH
 
 
@@ -98,10 +99,13 @@ def tile_blockmlp_mixerblock_pa_t_kernel(tc, y0, W1, b1, W2, b2, out):
         def regroup_z(unit, copy):
             pair, block = divmod(unit, BLOCKS)
             z_grouped = stage.tile([P, UNIT_TOKENS, PACK], BF16, align_bytes=64, bufs=3)
-            copy(
-                out=z_grouped[:].rearrange("p (g c) j -> p g c j", g=UNIT_GROUPS),
-                in_=y_raw[pair][:].rearrange("p g (j c n) -> p n g c j", j=PACK, n=BLOCKS)[:, block],
-            )
+            for g in range(UNIT_GROUPS):
+                copy(
+                    out=z_grouped[:, g * GROUP_TOKENS : (g + 1) * GROUP_TOKENS, :].rearrange(
+                        "p (c i) j -> p c j i", i=RUN
+                    ),
+                    in_=y_raw[pair][:, g, :].rearrange("p (j c i n) -> p n c j i", j=PACK, i=RUN, n=BLOCKS)[:, block],
+                )
             z_grouped_of[unit] = z_grouped
 
         def quantise(grouped, name, bufs):
@@ -129,7 +133,7 @@ def tile_blockmlp_mixerblock_pa_t_kernel(tc, y0, W1, b1, W2, b2, out):
 
         def gelu(unit):
             block = unit % BLOCKS
-            h_planes = stage.tile([P, PACK, UNIT_TOKENS], BF16, bufs=3)
+            h_planes = stage.tile([P, PACK, UNIT_TOKENS], BF16)
             for t in range(PACK):
                 nc.scalar.activation(
                     out=h_planes[:, t, :],
@@ -140,9 +144,12 @@ def tile_blockmlp_mixerblock_pa_t_kernel(tc, y0, W1, b1, W2, b2, out):
                 )
             h_planes_of[unit] = h_planes
 
-        def regroup_h(unit, copy):
+        def regroup_h(unit):
             h_grouped = stage.tile([P, UNIT_TOKENS, PACK], BF16, align_bytes=64)
-            copy(out=h_grouped[:], in_=h_planes_of[unit][:].rearrange("p t c -> p c t"))
+            nc.vector.tensor_copy(
+                out=h_grouped[:].rearrange("p (c i) t -> p c t i", i=RUN),
+                in_=h_planes_of[unit][:].rearrange("p t (c i) -> p c t i", i=RUN),
+            )
             h_grouped_of[unit] = h_grouped
 
         def layer2_passes(group, s):
@@ -171,7 +178,7 @@ def tile_blockmlp_mixerblock_pa_t_kernel(tc, y0, W1, b1, W2, b2, out):
                     in1=b2f[:, s, :].unsqueeze(1).to_broadcast([P, GROUP_TOKENS, BLOCKS]),
                     op=ADD,
                 )
-                nc.sync.dma_start(out=out_groups[group][:, s * WIDTH : (s + 1) * WIDTH], in_=rows[:, s, :])
+            nc.sync.dma_start(out=out_groups[group], in_=rows[:].rearrange("p s c -> p (s c)"))
 
         later_weights = [(1, 1), (2, 0), (2, 1)]
         prepare_weights(1, 0)
@@ -181,24 +188,23 @@ def tile_blockmlp_mixerblock_pa_t_kernel(tc, y0, W1, b1, W2, b2, out):
         for t in range(PACK):
             layer1_pass(0, t)
 
-        for step in range(UNITS + 2):
+        for step in range(UNITS + 3):
             if step + 1 < UNITS:
                 z_packed_of[step + 1] = quantise(z_grouped_of[step + 1], "z", 3)
             if step < len(later_weights):
                 prepare_weights(later_weights[step][0], later_weights[step][1])
             if 0 <= step - 1 < UNITS:
                 h_packed_of[step - 1] = quantise(h_grouped_of[step - 1], "h", 4)
+            if 0 <= step - 3 < GROUPS:
+                finish_group(step - 3)
             if step < UNITS:
                 gelu(step)
-                if step + 2 < UNITS:
-                    regroup_h(step, nc.vector.tensor_copy)
-                    regroup_z(step + 2, nc.scalar.copy)
-                else:
-                    regroup_h(step, nc.scalar.copy)
-            if step + 1 < UNITS:
-                for t in range(PACK):
-                    layer1_pass(step + 1, t)
-            if 0 <= step - 2 < GROUPS:
-                for s in range(PACK):
-                    layer2_passes(step - 2, s)
-                finish_group(step - 2)
+            for i in range(PACK):
+                if step + 1 < UNITS:
+                    layer1_pass(step + 1, i)
+                if 0 <= step - 2 < GROUPS:
+                    layer2_passes(step - 2, i)
+            if step < UNITS:
+                regroup_h(step)
+            if step + 2 < UNITS:
+                regroup_z(step + 2, nc.scalar.copy)

@@ -33,7 +33,6 @@ def tile_blockmlp_mixerblock_pa_t_kernel(tc, y0, W1, b1, W2, b2, out):
         stage = stack.enter_context(tc.tile_pool(name="stage", bufs=2))
         hidden_banks = stack.enter_context(tc.psum_pool(name="hidden_banks", bufs=4))
         out_banks = stack.enter_context(tc.psum_pool(name="out_banks", bufs=4))
-        stack.enter_context(tc.manual_schedule())
 
         b1_raw = keep.tile([P, BLOCKS, PACK], BF16)
         b2_raw = keep.tile([P, BLOCKS, PACK], BF16)

@@ -14,76 +14,81 @@ P = 128
 PACK = 4
 WIDTH = P * PACK
 BLOCKS = 2
+LAYERS = 2
 GROUPS = 16
 GROUP_TOKENS = WIDTH // BLOCKS
 UNIT_GROUPS = 2
 UNIT_TOKENS = UNIT_GROUPS * GROUP_TOKENS
 UNITS = GROUPS * BLOCKS // UNIT_GROUPS
+PAIRS = GROUPS // UNIT_GROUPS
 RUN = 4
-FLOPS = 2 * 2 * GROUPS * WIDTH * WIDTH * WIDTH
+DEPTH = {"z_grouped": 4, "z_packed": 3, "h_planes": 3, "h_grouped": 4, "h_packed": 5, "out_rows": 4, "w_grouped": 3}
+PSUM_BANKS_A_LAYER = 4
+FLOPS = 2 * LAYERS * GROUPS * WIDTH * WIDTH * WIDTH
 
 
 def tile_blockmlp_mixerblock_pa_t_kernel(tc, y0, W1, b1, W2, b2, out):
     nc = tc.nc
-    y_pairs = y0.rearrange("(q g p r) w -> q p g (r w)", g=UNIT_GROUPS, p=P, r=2)
+    y_groups = y0.rearrange("(g p r) w -> g p (r w)", p=P, r=2)
     out_groups = out.rearrange("(g p r) w -> g p (r w)", p=P, r=2)
+    weights = (W1, W2)
 
     with ExitStack() as stack:
         keep = stack.enter_context(tc.tile_pool(name="keep", bufs=1))
-        stage = stack.enter_context(tc.tile_pool(name="stage", bufs=2))
-        hidden_banks = stack.enter_context(tc.psum_pool(name="hidden_banks", bufs=4))
-        out_banks = stack.enter_context(tc.psum_pool(name="out_banks", bufs=4))
+        stage = stack.enter_context(tc.tile_pool(name="stage", bufs=1))
+        hidden_psum = stack.enter_context(tc.psum_pool(name="hidden_psum", bufs=PSUM_BANKS_A_LAYER))
+        out_psum = stack.enter_context(tc.psum_pool(name="out_psum", bufs=PSUM_BANKS_A_LAYER))
+
+        w_raw = {}
+        y_raw = {}
+
+        def load_weights(layer, block):
+            raw = keep.tile([P, PACK, WIDTH], BF16, name="w_raw%d%d" % (layer, block))
+            nc.sync.dma_start(out=raw[:], in_=weights[layer][block].rearrange("(p j) h -> p j h", j=PACK))
+            w_raw[(layer, block)] = raw
+
+        def load_pair(pair):
+            raw = keep.tile([P, UNIT_GROUPS, PACK * WIDTH], BF16, name="y_raw%d" % pair)
+            for g in range(UNIT_GROUPS):
+                nc.sync.dma_start(out=raw[:, g, :], in_=y_groups[pair * UNIT_GROUPS + g])
+            y_raw[pair] = raw
+
+        load_weights(0, 0)
+        load_pair(0)
+        load_weights(0, 1)
+        load_pair(1)
+        load_weights(1, 0)
+        load_weights(1, 1)
+        for pair in range(2, PAIRS):
+            load_pair(pair)
 
         b1_raw = keep.tile([P, BLOCKS, PACK], BF16)
         b2_raw = keep.tile([P, BLOCKS, PACK], BF16)
         nc.scalar.dma_start(out=b1_raw[:], in_=b1.rearrange("n o (m t) -> m (n o) t", t=PACK))
         nc.scalar.dma_start(out=b2_raw[:], in_=b2.rearrange("n o (m t) -> m (n o) t", t=PACK))
+        b1_f32 = keep.tile([P, BLOCKS, PACK], F32)
+        b2_f32 = keep.tile([P, PACK, BLOCKS], F32)
+        nc.vector.tensor_copy(out=b1_f32[:], in_=b1_raw[:])
+        nc.vector.tensor_copy(out=b2_f32[:], in_=b2_raw[:].rearrange("p n s -> p s n"))
 
-        w_raw = {}
-        y_raw = {}
+        dummy = keep.tile([P, 1], F32)
+        nc.vector.memset(dummy[:], 0.0)
+        nc.scalar.activation(out=dummy[:], in_=dummy[:], func=GELU)
 
-        def load_weights(layer, w, block):
-            raw = keep.tile([P, PACK, WIDTH], BF16, name="w_raw%d%d" % (layer, block))
-            nc.sync.dma_start(out=raw[:], in_=w[block].rearrange("(p j) h -> p j h", j=PACK))
-            w_raw[(layer, block)] = raw
+        w_words = {}
+        w_planes = {}
+        for layer in range(LAYERS):
+            w_words[layer] = keep.tile([P, BLOCKS, WIDTH], U32, name="w_words%d" % layer, align_bytes=64)
+            w_planes[layer] = keep.tile([P, BLOCKS, WIDTH], U8, name="w_planes%d" % layer, align_bytes=64)
 
-        def load_pair(pair):
-            raw = keep.tile([P, UNIT_GROUPS, PACK * WIDTH], BF16, name="y_raw%d" % pair)
-            nc.sync.dma_start(out=raw[:], in_=y_pairs[pair])
-            y_raw[pair] = raw
-
-        load_weights(1, W1, 0)
-        load_pair(0)
-        load_weights(1, W1, 1)
-        load_pair(1)
-        load_weights(2, W2, 0)
-        load_weights(2, W2, 1)
-        for pair in range(2, GROUPS // UNIT_GROUPS):
-            load_pair(pair)
-
-        warm = keep.tile([P, 1], F32)
-        nc.vector.memset(warm[:], 0.0)
-        nc.scalar.activation(out=warm[:], in_=warm[:], func=GELU)
-
-        b1f = keep.tile([P, BLOCKS, PACK], F32)
-        b2f = keep.tile([P, PACK, BLOCKS], F32)
-        nc.vector.tensor_copy(out=b1f[:], in_=b1_raw[:])
-        nc.vector.tensor_copy(out=b2f[:], in_=b2_raw[:].rearrange("p n s -> p s n"))
-
-        w_codes = {}
-        w_scales = {}
-        for layer in (1, 2):
-            w_codes[layer] = keep.tile([P, BLOCKS, WIDTH], U32, name="w_codes%d" % layer, align_bytes=64)
-            w_scales[layer] = keep.tile([P, BLOCKS, WIDTH], U8, name="w_scales%d" % layer, align_bytes=64)
-
-        def prepare_weights(layer, block):
-            w_grouped = stage.tile([P, PACK, P, PACK], BF16, align_bytes=64)
-            nc.vector.tensor_copy(
-                out=w_grouped[:], in_=w_raw[(layer, block)][:].rearrange("p j (m t) -> p t m j", t=PACK)
-            )
+        def prepare_weights(index):
+            layer, block = divmod(index, BLOCKS)
+            copy = nc.scalar.copy if layer == 0 else nc.vector.tensor_copy
+            w_grouped = stage.tile([P, PACK, P, PACK], BF16, align_bytes=64, bufs=DEPTH["w_grouped"])
+            copy(out=w_grouped[:], in_=w_raw[(layer, block)][:].rearrange("p j (m t) -> p t m j", t=PACK))
             nc.vector.quantize_mx(
-                out=w_codes[layer][:, block, :].bitcast(FP8X4),
-                scales=w_scales[layer][:, block, :],
+                out=w_words[layer][:, block, :].bitcast(FP8X4),
+                scales=w_planes[layer][:, block, :],
                 in_=w_grouped[:].rearrange("p t m j -> p (t m j)"),
             )
 
@@ -95,9 +100,10 @@ def tile_blockmlp_mixerblock_pa_t_kernel(tc, y0, W1, b1, W2, b2, out):
         h_packed_of = {}
         out_banks_of = {}
 
-        def regroup_z(unit, copy):
+        def regroup_z(unit):
             pair, block = divmod(unit, BLOCKS)
-            z_grouped = stage.tile([P, UNIT_TOKENS, PACK], BF16, align_bytes=64, bufs=3)
+            copy = nc.vector.tensor_copy if pair == 0 else nc.scalar.copy
+            z_grouped = stage.tile([P, UNIT_TOKENS, PACK], BF16, align_bytes=64, bufs=DEPTH["z_grouped"])
             for g in range(UNIT_GROUPS):
                 copy(
                     out=z_grouped[:, g * GROUP_TOKENS : (g + 1) * GROUP_TOKENS, :].rearrange(
@@ -107,24 +113,24 @@ def tile_blockmlp_mixerblock_pa_t_kernel(tc, y0, W1, b1, W2, b2, out):
                 )
             z_grouped_of[unit] = z_grouped
 
-        def quantise(grouped, name, bufs):
-            codes = stage.tile([P, UNIT_TOKENS], U32, align_bytes=64, name=name + "_codes", bufs=bufs)
-            scales = stage.tile([P, UNIT_TOKENS], U8, align_bytes=64, name=name + "_scales", bufs=bufs)
+        def quantise(grouped, name):
+            words = stage.tile([P, UNIT_TOKENS], U32, align_bytes=64, name=name + "_words", bufs=DEPTH[name])
+            plane = stage.tile([P, UNIT_TOKENS], U8, align_bytes=64, name=name + "_plane", bufs=DEPTH[name])
             nc.vector.quantize_mx(
-                out=codes[:].bitcast(FP8X4), scales=scales[:], in_=grouped[:].rearrange("p c j -> p (c j)")
+                out=words[:].bitcast(FP8X4), scales=plane[:], in_=grouped[:].rearrange("p c j -> p (c j)")
             )
-            return codes, scales
+            return words, plane
 
         def layer1_pass(unit, t):
             block = unit % BLOCKS
-            codes, scales = z_packed_of[unit]
-            bank = hidden_banks.tile([P, UNIT_TOKENS], F32)
+            words, plane = z_packed_of[unit]
+            bank = hidden_psum.tile([P, UNIT_TOKENS], F32)
             nc.tensor.matmul_mx(
                 out=bank[:],
-                lhsT=w_codes[1][:, block, t * P : (t + 1) * P].bitcast(FP8X4),
-                lhsT_scale=w_scales[1][:, block, t * P : (t + 1) * P],
-                rhs=codes[:].bitcast(FP8X4),
-                rhs_scale=scales[:],
+                lhsT=w_words[0][:, block, t * P : (t + 1) * P].bitcast(FP8X4),
+                lhsT_scale=w_planes[0][:, block, t * P : (t + 1) * P],
+                rhs=words[:].bitcast(FP8X4),
+                rhs_scale=plane[:],
                 start=True,
                 stop=True,
             )
@@ -132,20 +138,20 @@ def tile_blockmlp_mixerblock_pa_t_kernel(tc, y0, W1, b1, W2, b2, out):
 
         def gelu(unit):
             block = unit % BLOCKS
-            h_planes = stage.tile([P, PACK, UNIT_TOKENS], BF16)
+            h_planes = stage.tile([P, PACK, UNIT_TOKENS], BF16, bufs=DEPTH["h_planes"])
             for t in range(PACK):
                 nc.scalar.activation(
                     out=h_planes[:, t, :],
                     in_=hidden_banks_of[(unit, t)][:],
                     func=GELU,
-                    bias=b1f[:, block, t : t + 1],
+                    bias=b1_f32[:, block, t : t + 1],
                     scale=1.0,
                 )
             h_planes_of[unit] = h_planes
 
-        def regroup_h(unit):
-            h_grouped = stage.tile([P, UNIT_TOKENS, PACK], BF16, align_bytes=64)
-            nc.vector.tensor_copy(
+        def regroup_h(unit, copy):
+            h_grouped = stage.tile([P, UNIT_TOKENS, PACK], BF16, align_bytes=64, bufs=DEPTH["h_grouped"])
+            copy(
                 out=h_grouped[:].rearrange("p (c i) t -> p c t i", i=RUN),
                 in_=h_planes_of[unit][:].rearrange("p t (c i) -> p c t i", i=RUN),
             )
@@ -154,46 +160,45 @@ def tile_blockmlp_mixerblock_pa_t_kernel(tc, y0, W1, b1, W2, b2, out):
         def layer2_passes(group, s):
             pair, half = divmod(group, UNIT_GROUPS)
             tokens = slice(half * GROUP_TOKENS, (half + 1) * GROUP_TOKENS)
-            bank = out_banks.tile([P, BLOCKS, GROUP_TOKENS], F32)
+            bank = out_psum.tile([P, BLOCKS, GROUP_TOKENS], F32)
             for block in range(BLOCKS):
-                codes, scales = h_packed_of[pair * BLOCKS + block]
+                words, plane = h_packed_of[pair * BLOCKS + block]
                 nc.tensor.matmul_mx(
                     out=bank[:, block, :],
-                    lhsT=w_codes[2][:, block, s * P : (s + 1) * P].bitcast(FP8X4),
-                    lhsT_scale=w_scales[2][:, block, s * P : (s + 1) * P],
-                    rhs=codes[:, tokens].bitcast(FP8X4),
-                    rhs_scale=scales[:, tokens],
+                    lhsT=w_words[1][:, block, s * P : (s + 1) * P].bitcast(FP8X4),
+                    lhsT_scale=w_planes[1][:, block, s * P : (s + 1) * P],
+                    rhs=words[:, tokens].bitcast(FP8X4),
+                    rhs_scale=plane[:, tokens],
                     start=True,
                     stop=True,
                 )
             out_banks_of[(group, s)] = bank
 
         def finish_group(group):
-            rows = stage.tile([P, PACK, WIDTH], F32, bufs=3)
+            out_rows = stage.tile([P, PACK, WIDTH], F32, bufs=DEPTH["out_rows"])
             for s in range(PACK):
                 nc.vector.tensor_tensor(
-                    out=rows[:, s, :].rearrange("p (c n) -> p c n", n=BLOCKS),
+                    out=out_rows[:, s, :].rearrange("p (c n) -> p c n", n=BLOCKS),
                     in0=out_banks_of[(group, s)][:].rearrange("p n c -> p c n"),
-                    in1=b2f[:, s, :].unsqueeze(1).to_broadcast([P, GROUP_TOKENS, BLOCKS]),
+                    in1=b2_f32[:, s, :].unsqueeze(1).to_broadcast([P, GROUP_TOKENS, BLOCKS]),
                     op=ADD,
                 )
-            nc.sync.dma_start(out=out_groups[group], in_=rows[:].rearrange("p s c -> p (s c)"))
+                nc.sync.dma_start(out=out_groups[group][:, s * WIDTH : (s + 1) * WIDTH], in_=out_rows[:, s, :])
 
-        later_weights = [(1, 1), (2, 0), (2, 1)]
-        prepare_weights(1, 0)
-        regroup_z(0, nc.vector.tensor_copy)
-        regroup_z(1, nc.scalar.copy)
-        z_packed_of[0] = quantise(z_grouped_of[0], "z", 3)
+        prepare_weights(0)
+        regroup_z(0)
+        regroup_z(1)
+        z_packed_of[0] = quantise(z_grouped_of[0], "z_packed")
         for t in range(PACK):
             layer1_pass(0, t)
 
         for step in range(UNITS + 3):
             if step + 1 < UNITS:
-                z_packed_of[step + 1] = quantise(z_grouped_of[step + 1], "z", 3)
-            if step < len(later_weights):
-                prepare_weights(later_weights[step][0], later_weights[step][1])
+                z_packed_of[step + 1] = quantise(z_grouped_of[step + 1], "z_packed")
+            if step + 1 < LAYERS * BLOCKS:
+                prepare_weights(step + 1)
             if 0 <= step - 1 < UNITS:
-                h_packed_of[step - 1] = quantise(h_grouped_of[step - 1], "h", 4)
+                h_packed_of[step - 1] = quantise(h_grouped_of[step - 1], "h_packed")
             if 0 <= step - 3 < GROUPS:
                 finish_group(step - 3)
             if step < UNITS:
@@ -203,7 +208,8 @@ def tile_blockmlp_mixerblock_pa_t_kernel(tc, y0, W1, b1, W2, b2, out):
                     layer1_pass(step + 1, i)
                 if 0 <= step - 2 < GROUPS:
                     layer2_passes(step - 2, i)
-            if step < UNITS:
-                regroup_h(step)
             if step + 2 < UNITS:
-                regroup_z(step + 2, nc.scalar.copy)
+                regroup_h(step, nc.vector.tensor_copy)
+                regroup_z(step + 2)
+            elif step < UNITS:
+                regroup_h(step, nc.scalar.copy)

@@ -9,6 +9,7 @@ U8 = mybir.dt.uint8
 FP8X4 = mybir.dt.float8_e4m3fn_x4
 GELU = mybir.ActivationFunctionType.Gelu
 ADD = mybir.AluOpType.add
+MULT = mybir.AluOpType.mult
 
 P = 128
 PACK = 4
@@ -22,7 +23,7 @@ UNIT_TOKENS = UNIT_GROUPS * GROUP_TOKENS
 UNITS = GROUPS * BLOCKS // UNIT_GROUPS
 PAIRS = GROUPS // UNIT_GROUPS
 RUN = 4
-DEPTH = {"z_grouped": 4, "z_packed": 3, "h_planes": 3, "h_grouped": 4, "h_packed": 5, "out_rows": 4, "w_grouped": 3}
+DEPTH = {"z_grouped": 2, "z_packed": 3, "h_planes": 3, "h_grouped": 4, "h_packed": 5, "out_rows": 4, "w_grouped": 3}
 PSUM_BANKS_A_LAYER = 4
 FLOPS = 2 * LAYERS * GROUPS * WIDTH * WIDTH * WIDTH
 
@@ -66,13 +67,8 @@ def tile_blockmlp_mixerblock_pa_t_kernel(tc, y0, W1, b1, W2, b2, out):
         b2_raw = keep.tile([P, BLOCKS, PACK], BF16)
         nc.scalar.dma_start(out=b1_raw[:], in_=b1.rearrange("n o (m t) -> m (n o) t", t=PACK))
         nc.scalar.dma_start(out=b2_raw[:], in_=b2.rearrange("n o (m t) -> m (n o) t", t=PACK))
-        b1_f32 = keep.tile([P, BLOCKS, PACK], F32)
-        b2_f32 = keep.tile([P, PACK, BLOCKS], F32)
-        nc.vector.tensor_copy(out=b1_f32[:], in_=b1_raw[:])
-        nc.vector.tensor_copy(out=b2_f32[:], in_=b2_raw[:].rearrange("p n s -> p s n"))
-
         dummy = keep.tile([P, 1], F32)
-        nc.vector.memset(dummy[:], 0.0)
+        nc.gpsimd.memset(dummy[:], 0.0)
         nc.scalar.activation(out=dummy[:], in_=dummy[:], func=GELU)
 
         w_words = {}
@@ -81,11 +77,15 @@ def tile_blockmlp_mixerblock_pa_t_kernel(tc, y0, W1, b1, W2, b2, out):
             w_words[layer] = keep.tile([P, BLOCKS, WIDTH], U32, name="w_words%d" % layer, align_bytes=64)
             w_planes[layer] = keep.tile([P, BLOCKS, WIDTH], U8, name="w_planes%d" % layer, align_bytes=64)
 
-        def prepare_weights(index):
-            layer, block = divmod(index, BLOCKS)
-            copy = nc.scalar.copy if layer == 0 else nc.vector.tensor_copy
+        def prepare_weights(layer, block, shares):
             w_grouped = stage.tile([P, PACK, P, PACK], BF16, align_bytes=64, bufs=DEPTH["w_grouped"])
-            copy(out=w_grouped[:], in_=w_raw[(layer, block)][:].rearrange("p j (m t) -> p t m j", t=PACK))
+            first = 0
+            for copy, count in shares:
+                copy(
+                    out=w_grouped[:, first : first + count],
+                    in_=w_raw[(layer, block)][:].rearrange("p j (m t) -> p t m j", t=PACK)[:, first : first + count],
+                )
+                first += count
             nc.vector.quantize_mx(
                 out=w_words[layer][:, block, :].bitcast(FP8X4),
                 scales=w_planes[layer][:, block, :],
@@ -99,63 +99,94 @@ def tile_blockmlp_mixerblock_pa_t_kernel(tc, y0, W1, b1, W2, b2, out):
         h_grouped_of = {}
         h_packed_of = {}
         out_banks_of = {}
+        out_rows_of = {}
 
-        def regroup_z(unit):
+        def slices_of(unit):
+            if unit in (0, UNITS - 1):
+                return [slice(g * GROUP_TOKENS, (g + 1) * GROUP_TOKENS) for g in range(UNIT_GROUPS)]
+            return [slice(0, UNIT_TOKENS)]
+
+        def regroup_z(unit, g, copy):
             pair, block = divmod(unit, BLOCKS)
-            copy = nc.vector.tensor_copy if pair == 0 else nc.scalar.copy
-            z_grouped = stage.tile([P, UNIT_TOKENS, PACK], BF16, align_bytes=64, bufs=DEPTH["z_grouped"])
-            for g in range(UNIT_GROUPS):
-                copy(
-                    out=z_grouped[:, g * GROUP_TOKENS : (g + 1) * GROUP_TOKENS, :].rearrange(
-                        "p (c i) j -> p c j i", i=RUN
-                    ),
-                    in_=y_raw[pair][:, g, :].rearrange("p (j c i n) -> p n c j i", j=PACK, i=RUN, n=BLOCKS)[:, block],
-                )
-            z_grouped_of[unit] = z_grouped
-
-        def quantise(grouped, name):
-            words = stage.tile([P, UNIT_TOKENS], U32, align_bytes=64, name=name + "_words", bufs=DEPTH[name])
-            plane = stage.tile([P, UNIT_TOKENS], U8, align_bytes=64, name=name + "_plane", bufs=DEPTH[name])
-            nc.vector.quantize_mx(
-                out=words[:].bitcast(FP8X4), scales=plane[:], in_=grouped[:].rearrange("p c j -> p (c j)")
+            if unit not in z_grouped_of:
+                z_grouped = stage.tile([P, UNIT_TOKENS, PACK], BF16, align_bytes=64, bufs=DEPTH["z_grouped"])
+                z_grouped_of[unit] = z_grouped
+            copy(
+                out=z_grouped_of[unit][:, g * GROUP_TOKENS : (g + 1) * GROUP_TOKENS, :].rearrange(
+                    "p (c i) j -> p c j i", i=RUN
+                ),
+                in_=y_raw[pair][:, g, :].rearrange("p (j c i n) -> p n c j i", j=PACK, i=RUN, n=BLOCKS)[:, block],
             )
-            return words, plane
 
-        def layer1_pass(unit, t):
+        def regroup_z_on_gpsimd(unit, g):
+            pair, block = divmod(unit, BLOCKS)
+            if unit not in z_grouped_of:
+                z_grouped = stage.tile([P, UNIT_TOKENS, PACK], BF16, align_bytes=64, bufs=DEPTH["z_grouped"])
+                z_grouped_of[unit] = z_grouped
+            nc.gpsimd.tensor_scalar(
+                out=z_grouped_of[unit][:, g * GROUP_TOKENS : (g + 1) * GROUP_TOKENS, :],
+                in0=y_raw[pair][:, g, :].rearrange("p (j c n) -> p n c j", j=PACK, n=BLOCKS)[:, block],
+                scalar1=1.0,
+                scalar2=0.0,
+                op0=MULT,
+                op1=ADD,
+            )
+
+        def quantise(unit, tokens, grouped_of, packed_of, name):
+            if unit not in packed_of:
+                words = stage.tile([P, UNIT_TOKENS], U32, align_bytes=64, name=name + "_words", bufs=DEPTH[name])
+                plane = stage.tile([P, UNIT_TOKENS], U8, align_bytes=64, name=name + "_plane", bufs=DEPTH[name])
+                packed_of[unit] = (words, plane)
+            words, plane = packed_of[unit]
+            nc.vector.quantize_mx(
+                out=words[:, tokens].bitcast(FP8X4),
+                scales=plane[:, tokens],
+                in_=grouped_of[unit][:, tokens, :].rearrange("p c j -> p (c j)"),
+            )
+
+        def quantise_z(unit, tokens):
+            quantise(unit, tokens, z_grouped_of, z_packed_of, "z_packed")
+
+        def quantise_h(unit, tokens):
+            quantise(unit, tokens, h_grouped_of, h_packed_of, "h_packed")
+
+        def layer1_pass(unit, tokens, t):
             block = unit % BLOCKS
             words, plane = z_packed_of[unit]
             bank = hidden_psum.tile([P, UNIT_TOKENS], F32)
             nc.tensor.matmul_mx(
-                out=bank[:],
+                out=bank[:, : tokens.stop - tokens.start],
                 lhsT=w_words[0][:, block, t * P : (t + 1) * P].bitcast(FP8X4),
                 lhsT_scale=w_planes[0][:, block, t * P : (t + 1) * P],
-                rhs=words[:].bitcast(FP8X4),
-                rhs_scale=plane[:],
+                rhs=words[:, tokens].bitcast(FP8X4),
+                rhs_scale=plane[:, tokens],
                 start=True,
                 stop=True,
             )
-            hidden_banks_of[(unit, t)] = bank
+            hidden_banks_of[(unit, tokens.start, t)] = bank
 
-        def gelu(unit):
+        def gelu(unit, tokens):
             block = unit % BLOCKS
-            h_planes = stage.tile([P, PACK, UNIT_TOKENS], BF16, bufs=DEPTH["h_planes"])
+            if unit not in h_planes_of:
+                h_planes = stage.tile([P, PACK, UNIT_TOKENS], BF16, bufs=DEPTH["h_planes"])
+                h_planes_of[unit] = h_planes
             for t in range(PACK):
                 nc.scalar.activation(
-                    out=h_planes[:, t, :],
-                    in_=hidden_banks_of[(unit, t)][:],
+                    out=h_planes_of[unit][:, t, tokens],
+                    in_=hidden_banks_of[(unit, tokens.start, t)][:, : tokens.stop - tokens.start],
                     func=GELU,
-                    bias=b1_f32[:, block, t : t + 1],
+                    bias=b1_raw[:, block, t : t + 1],
                     scale=1.0,
                 )
-            h_planes_of[unit] = h_planes
 
-        def regroup_h(unit, copy):
-            h_grouped = stage.tile([P, UNIT_TOKENS, PACK], BF16, align_bytes=64, bufs=DEPTH["h_grouped"])
+        def regroup_h(unit, tokens, copy):
+            if unit not in h_grouped_of:
+                h_grouped = stage.tile([P, UNIT_TOKENS, PACK], BF16, align_bytes=64, bufs=DEPTH["h_grouped"])
+                h_grouped_of[unit] = h_grouped
             copy(
-                out=h_grouped[:].rearrange("p (c i) t -> p c t i", i=RUN),
-                in_=h_planes_of[unit][:].rearrange("p t (c i) -> p c t i", i=RUN),
+                out=h_grouped_of[unit][:, tokens, :].rearrange("p (c i) t -> p c t i", i=RUN),
+                in_=h_planes_of[unit][:, :, tokens].rearrange("p t (c i) -> p c t i", i=RUN),
             )
-            h_grouped_of[unit] = h_grouped
 
         def layer2_passes(group, s):
             pair, half = divmod(group, UNIT_GROUPS)
@@ -174,42 +205,73 @@ def tile_blockmlp_mixerblock_pa_t_kernel(tc, y0, W1, b1, W2, b2, out):
                 )
             out_banks_of[(group, s)] = bank
 
-        def finish_group(group):
-            out_rows = stage.tile([P, PACK, WIDTH], F32, bufs=DEPTH["out_rows"])
-            for s in range(PACK):
-                nc.vector.tensor_tensor(
-                    out=out_rows[:, s, :].rearrange("p (c n) -> p c n", n=BLOCKS),
-                    in0=out_banks_of[(group, s)][:].rearrange("p n c -> p c n"),
-                    in1=b2_f32[:, s, :].unsqueeze(1).to_broadcast([P, GROUP_TOKENS, BLOCKS]),
-                    op=ADD,
-                )
-                nc.sync.dma_start(out=out_groups[group][:, s * WIDTH : (s + 1) * WIDTH], in_=out_rows[:, s, :])
+        def finish_slice(group, s):
+            if group not in out_rows_of:
+                out_rows = stage.tile([P, PACK, WIDTH], F32, bufs=DEPTH["out_rows"])
+                out_rows_of[group] = out_rows
+            out_rows = out_rows_of[group]
+            nc.vector.tensor_tensor(
+                out=out_rows[:, s, :].rearrange("p (c n) -> p c n", n=BLOCKS),
+                in0=out_banks_of[(group, s)][:].rearrange("p n c -> p c n"),
+                in1=b2_raw[:, :, s].unsqueeze(1).to_broadcast([P, GROUP_TOKENS, BLOCKS]),
+                op=ADD,
+            )
+            nc.sync.dma_start(out=out_groups[group][:, s * WIDTH : (s + 1) * WIDTH], in_=out_rows[:, s, :])
 
-        prepare_weights(0)
-        regroup_z(0)
-        regroup_z(1)
-        z_packed_of[0] = quantise(z_grouped_of[0], "z_packed")
-        for t in range(PACK):
-            layer1_pass(0, t)
+        on_vector = nc.vector.tensor_copy
+        on_scalar = nc.scalar.copy
+        prepare_weights(0, 0, [(on_vector, 4)])
+        regroup_z(0, 0, on_scalar)
+        regroup_z(0, 1, on_vector)
+        for tokens in slices_of(0):
+            quantise_z(0, tokens)
+            for t in range(PACK):
+                layer1_pass(0, tokens, t)
+        regroup_z(1, 0, on_vector)
+        regroup_z(1, 1, on_scalar)
+        prepare_weights(0, 1, [(on_vector, 4)])
 
-        for step in range(UNITS + 3):
+        def z_stage(unit):
+            if unit < UNITS:
+                regroup_z_on_gpsimd(unit, 0)
+                regroup_z(unit, 1, on_scalar)
+
+        z_stage(2)
+
+        def one_step(step):
             if step + 1 < UNITS:
-                z_packed_of[step + 1] = quantise(z_grouped_of[step + 1], "z_packed")
-            if step + 1 < LAYERS * BLOCKS:
-                prepare_weights(step + 1)
+                for tokens in slices_of(step + 1):
+                    quantise_z(step + 1, tokens)
+            if step in (1, 2):
+                prepare_weights(1, step - 1, [(on_vector, 4)])
             if 0 <= step - 1 < UNITS:
-                h_packed_of[step - 1] = quantise(h_grouped_of[step - 1], "h_packed")
+                for tokens in slices_of(step - 1):
+                    quantise_h(step - 1, tokens)
             if 0 <= step - 3 < GROUPS:
-                finish_group(step - 3)
+                for s in range(PACK):
+                    finish_slice(step - 3, s)
             if step < UNITS:
-                gelu(step)
+                for tokens in slices_of(step):
+                    gelu(step, tokens)
+            for tokens in slices_of(step + 1) if step + 1 == UNITS - 1 else []:
+                for t in range(PACK):
+                    layer1_pass(step + 1, tokens, t)
             for i in range(PACK):
-                if step + 1 < UNITS:
-                    layer1_pass(step + 1, i)
+                if step + 1 < UNITS - 1:
+                    layer1_pass(step + 1, slice(0, UNIT_TOKENS), i)
                 if 0 <= step - 2 < GROUPS:
                     layer2_passes(step - 2, i)
-            if step + 2 < UNITS:
-                regroup_h(step, nc.vector.tensor_copy)
-                regroup_z(step + 2)
-            elif step < UNITS:
-                regroup_h(step, nc.scalar.copy)
+            if step < UNITS:
+                for tokens in slices_of(step):
+                    cut = tokens.start + (tokens.stop - tokens.start) * 5 // 8
+                    regroup_h(step, slice(tokens.start, cut), on_vector)
+                    regroup_h(step, slice(cut, tokens.stop), on_scalar)
+            z_stage(step + 3)
+
+        for step in range(2):
+            one_step(step)
+        with tc.manual_schedule(engines={mybir.EngineType.DVE, mybir.EngineType.Pool}):
+            for step in range(2, UNITS):
+                one_step(step)
+        for step in range(UNITS, UNITS + 3):
+            one_step(step)

@@ -9,7 +9,6 @@ U8 = mybir.dt.uint8
 FP8X4 = mybir.dt.float8_e4m3fn_x4
 GELU = mybir.ActivationFunctionType.Gelu
 ADD = mybir.AluOpType.add
-MULT = mybir.AluOpType.mult
 
 P = 128
 PACK = 4
@@ -23,7 +22,7 @@ UNIT_TOKENS = UNIT_GROUPS * GROUP_TOKENS
 UNITS = GROUPS * BLOCKS // UNIT_GROUPS
 PAIRS = GROUPS // UNIT_GROUPS
 RUN = 4
-DEPTH = {"z_grouped": 2, "z_packed": 3, "h_planes": 3, "h_grouped": 4, "h_packed": 5, "out_rows": 4, "w_grouped": 3}
+DEPTH = {"z_grouped": 4, "z_packed": 3, "h_planes": 3, "h_grouped": 4, "h_packed": 5, "out_rows": 4, "w_grouped": 3}
 PSUM_BANKS_A_LAYER = 4
 FLOPS = 2 * LAYERS * GROUPS * WIDTH * WIDTH * WIDTH
 
@@ -116,20 +115,6 @@ def tile_blockmlp_mixerblock_pa_t_kernel(tc, y0, W1, b1, W2, b2, out):
                     "p (c i) j -> p c j i", i=RUN
                 ),
                 in_=y_raw[pair][:, g, :].rearrange("p (j c i n) -> p n c j i", j=PACK, i=RUN, n=BLOCKS)[:, block],
-            )
-
-        def regroup_z_on_gpsimd(unit, g):
-            pair, block = divmod(unit, BLOCKS)
-            if unit not in z_grouped_of:
-                z_grouped = stage.tile([P, UNIT_TOKENS, PACK], BF16, align_bytes=64, bufs=DEPTH["z_grouped"])
-                z_grouped_of[unit] = z_grouped
-            nc.gpsimd.tensor_scalar(
-                out=z_grouped_of[unit][:, g * GROUP_TOKENS : (g + 1) * GROUP_TOKENS, :],
-                in0=y_raw[pair][:, g, :].rearrange("p (j c n) -> p n c j", j=PACK, n=BLOCKS)[:, block],
-                scalar1=1.0,
-                scalar2=0.0,
-                op0=MULT,
-                op1=ADD,
             )
 
         def quantise(unit, tokens, grouped_of, packed_of, name):
@@ -233,10 +218,8 @@ def tile_blockmlp_mixerblock_pa_t_kernel(tc, y0, W1, b1, W2, b2, out):
 
         def z_stage(unit):
             if unit < UNITS:
-                regroup_z_on_gpsimd(unit, 0)
-                regroup_z(unit, 1, on_scalar)
-
-        z_stage(2)
+                for g in range(UNIT_GROUPS):
+                    regroup_z(unit, g, on_vector if unit < 3 else on_scalar)
 
         def one_step(step):
             if step + 1 < UNITS:
@@ -263,15 +246,13 @@ def tile_blockmlp_mixerblock_pa_t_kernel(tc, y0, W1, b1, W2, b2, out):
                     layer2_passes(step - 2, i)
             if step < UNITS:
                 for tokens in slices_of(step):
-                    cut = tokens.start + (tokens.stop - tokens.start) * 5 // 8
-                    regroup_h(step, slice(tokens.start, cut), on_vector)
-                    regroup_h(step, slice(cut, tokens.stop), on_scalar)
-            z_stage(step + 3)
+                    share = {UNITS - 2: 4, UNITS - 1: 0}.get(step, 8)
+                    cut = tokens.start + (tokens.stop - tokens.start) * share // 8
+                    if cut > tokens.start:
+                        regroup_h(step, slice(tokens.start, cut), on_vector)
+                    if cut < tokens.stop:
+                        regroup_h(step, slice(cut, tokens.stop), on_scalar)
+            z_stage(step + 2)
 
-        for step in range(2):
-            one_step(step)
-        with tc.manual_schedule(engines={mybir.EngineType.DVE, mybir.EngineType.Pool}):
-            for step in range(2, UNITS):
-                one_step(step)
-        for step in range(UNITS, UNITS + 3):
+        for step in range(UNITS + 3):
             one_step(step)

@@ -22,6 +22,7 @@ UNIT_TOKENS = UNIT_GROUPS * GROUP_TOKENS
 UNITS = GROUPS * BLOCKS // UNIT_GROUPS
 PAIRS = GROUPS // UNIT_GROUPS
 RUN = 4
+RUN_H = 8
 DEPTH = {"z_grouped": 4, "z_packed": 3, "h_planes": 3, "h_grouped": 4, "h_packed": 5, "out_rows": 4, "w_grouped": 3}
 PSUM_BANKS_A_LAYER = 4
 FLOPS = 2 * LAYERS * GROUPS * WIDTH * WIDTH * WIDTH
@@ -169,8 +170,8 @@ def tile_blockmlp_mixerblock_pa_t_kernel(tc, y0, W1, b1, W2, b2, out):
                 h_grouped = stage.tile([P, UNIT_TOKENS, PACK], BF16, align_bytes=64, bufs=DEPTH["h_grouped"])
                 h_grouped_of[unit] = h_grouped
             copy(
-                out=h_grouped_of[unit][:, tokens, :].rearrange("p (c i) t -> p c t i", i=RUN),
-                in_=h_planes_of[unit][:, :, tokens].rearrange("p t (c i) -> p c t i", i=RUN),
+                out=h_grouped_of[unit][:, tokens, :].rearrange("p (c i) t -> p c t i", i=RUN_H),
+                in_=h_planes_of[unit][:, :, tokens].rearrange("p t (c i) -> p c t i", i=RUN_H),
             )
 
         def layer2_passes(group, s):

@@ -1,6 +1,7 @@
 from contextlib import ExitStack
 
 import concourse.mybir as mybir
+from concourse.masks import make_identity
 
 BF16 = mybir.dt.bfloat16
 F32 = mybir.dt.float32
@@ -23,8 +24,8 @@ UNITS = GROUPS * BLOCKS // UNIT_GROUPS
 PAIRS = GROUPS // UNIT_GROUPS
 RUN = 4
 RUN_H = 8
-DEPTH = {"z_grouped": 4, "z_packed": 3, "h_planes": 3, "h_grouped": 4, "h_packed": 5, "out_rows": 4, "w_grouped": 3}
-PSUM_BANKS_A_LAYER = 4
+DEPTH = {"z_grouped": 4, "z_packed": 3, "h_planes": 3, "h_grouped": 4, "h_packed": 5, "w_grouped": 2}
+PSUM_BANKS = {"hidden": 4, "out": 3, "z": 1}
 FLOPS = 2 * LAYERS * GROUPS * WIDTH * WIDTH * WIDTH
 
 
@@ -37,8 +38,10 @@ def tile_blockmlp_mixerblock_pa_t_kernel(tc, y0, W1, b1, W2, b2, out):
     with ExitStack() as stack:
         keep = stack.enter_context(tc.tile_pool(name="keep", bufs=1))
         stage = stack.enter_context(tc.tile_pool(name="stage", bufs=1))
-        hidden_psum = stack.enter_context(tc.psum_pool(name="hidden_psum", bufs=PSUM_BANKS_A_LAYER))
-        out_psum = stack.enter_context(tc.psum_pool(name="out_psum", bufs=PSUM_BANKS_A_LAYER))
+        rows = stack.enter_context(tc.tile_pool(name="rows", bufs=PAIRS + GROUPS // 2))
+        hidden_psum = stack.enter_context(tc.psum_pool(name="hidden_psum", bufs=PSUM_BANKS["hidden"]))
+        z_psum = stack.enter_context(tc.psum_pool(name="z_psum", bufs=PSUM_BANKS["z"]))
+        out_psum = stack.enter_context(tc.psum_pool(name="out_psum", bufs=PSUM_BANKS["out"]))
 
         w_raw = {}
         y_raw = {}
@@ -49,7 +52,7 @@ def tile_blockmlp_mixerblock_pa_t_kernel(tc, y0, W1, b1, W2, b2, out):
             w_raw[(layer, block)] = raw
 
         def load_pair(pair):
-            raw = keep.tile([P, UNIT_GROUPS, PACK * WIDTH], BF16, name="y_raw%d" % pair)
+            raw = rows.tile([P, UNIT_GROUPS, PACK * WIDTH], BF16, tag="rows", name="y_raw%d" % pair)
             for g in range(UNIT_GROUPS):
                 nc.sync.dma_start(out=raw[:, g, :], in_=y_groups[pair * UNIT_GROUPS + g])
             y_raw[pair] = raw
@@ -67,6 +70,9 @@ def tile_blockmlp_mixerblock_pa_t_kernel(tc, y0, W1, b1, W2, b2, out):
         b2_raw = keep.tile([P, BLOCKS, PACK], BF16)
         nc.scalar.dma_start(out=b1_raw[:], in_=b1.rearrange("n o (m t) -> m (n o) t", t=PACK))
         nc.scalar.dma_start(out=b2_raw[:], in_=b2.rearrange("n o (m t) -> m (n o) t", t=PACK))
+        identity = keep.tile([P, P], BF16)
+        make_identity(nc, identity[:])
+
         dummy = keep.tile([P, 1], F32)
         nc.gpsimd.memset(dummy[:], 0.0)
         nc.scalar.activation(out=dummy[:], in_=dummy[:], func=GELU)
@@ -117,6 +123,16 @@ def tile_blockmlp_mixerblock_pa_t_kernel(tc, y0, W1, b1, W2, b2, out):
                 ),
                 in_=y_raw[pair][:, g, :].rearrange("p (j c i n) -> p n c j i", j=PACK, i=RUN, n=BLOCKS)[:, block],
             )
+
+        def regroup_z_through_psum(unit, g):
+            pair, block = divmod(unit, BLOCKS)
+            source = y_raw[pair][:, g, :].rearrange("p (j c n) -> p n j c", j=PACK, n=BLOCKS)[:, block]
+            bank = z_psum.tile([P, GROUP_TOKENS, PACK], BF16)
+            words = bank[:].bitcast(F32)
+            for j in (1, 3, 0, 2):
+                out_j = words[:, :, j // 2] if j % 2 else bank[:, :, j]
+                nc.tensor.matmul(out=out_j, lhsT=identity[:], rhs=source[:, j, :], start=True, stop=True)
+            nc.scalar.copy(out=z_grouped_of[unit][:, g * GROUP_TOKENS : (g + 1) * GROUP_TOKENS, :], in_=bank[:])
 
         def quantise(unit, tokens, grouped_of, packed_of, name):
             if unit not in packed_of:
@@ -193,7 +209,7 @@ def tile_blockmlp_mixerblock_pa_t_kernel(tc, y0, W1, b1, W2, b2, out):
 
         def finish_slice(group, s):
             if group not in out_rows_of:
-                out_rows = stage.tile([P, PACK, WIDTH], F32, bufs=DEPTH["out_rows"])
+                out_rows = rows.tile([P, PACK, WIDTH], F32, tag="rows", name="out_rows%d" % group)
                 out_rows_of[group] = out_rows
             out_rows = out_rows_of[group]
             nc.vector.tensor_tensor(
@@ -219,8 +235,11 @@ def tile_blockmlp_mixerblock_pa_t_kernel(tc, y0, W1, b1, W2, b2, out):
 
         def z_stage(unit):
             if unit < UNITS:
-                for g in range(UNIT_GROUPS):
-                    regroup_z(unit, g, on_vector if unit < 3 else on_scalar)
+                regroup_z(unit, 0, on_vector if unit < 3 else on_scalar)
+                if unit < 3:
+                    regroup_z(unit, 1, on_vector)
+                else:
+                    regroup_z_through_psum(unit, 1)
 
         def one_step(step):
             if step + 1 < UNITS:
@@ -247,7 +266,7 @@ def tile_blockmlp_mixerblock_pa_t_kernel(tc, y0, W1, b1, W2, b2, out):
                     layer2_passes(step - 2, i)
             if step < UNITS:
                 for tokens in slices_of(step):
-                    share = {UNITS - 2: 4, UNITS - 1: 0}.get(step, 8)
+                    share = 0 if step in (5, 10) or step >= UNITS - 2 else 8
                     cut = tokens.start + (tokens.stop - tokens.start) * share // 8
                     if cut > tokens.start:
                         regroup_h(step, slice(tokens.start, cut), on_vector)

@@ -25,7 +25,7 @@ PAIRS = GROUPS // UNIT_GROUPS
 RUN = 4
 RUN_H = 8
 DEPTH = {"z_grouped": 4, "z_packed": 3, "h_planes": 3, "h_grouped": 4, "h_packed": 5, "w_grouped": 2}
-PSUM_BANKS = {"hidden": 4, "out": 3, "z": 1}
+PSUM_BANKS = {"hidden": 3, "out": 3, "z": 2}
 FLOPS = 2 * LAYERS * GROUPS * WIDTH * WIDTH * WIDTH
 
 
@@ -127,12 +127,17 @@ def tile_blockmlp_mixerblock_pa_t_kernel(tc, y0, W1, b1, W2, b2, out):
         def regroup_z_through_psum(unit, g):
             pair, block = divmod(unit, BLOCKS)
             source = y_raw[pair][:, g, :].rearrange("p (j c n) -> p n j c", j=PACK, n=BLOCKS)[:, block]
-            bank = z_psum.tile([P, GROUP_TOKENS, PACK], BF16)
-            words = bank[:].bitcast(F32)
-            for j in (1, 3, 0, 2):
-                out_j = words[:, :, j // 2] if j % 2 else bank[:, :, j]
-                nc.tensor.matmul(out=out_j, lhsT=identity[:], rhs=source[:, j, :], start=True, stop=True)
-            nc.scalar.copy(out=z_grouped_of[unit][:, g * GROUP_TOKENS : (g + 1) * GROUP_TOKENS, :], in_=bank[:])
+            if unit not in z_grouped_of:
+                z_grouped = stage.tile([P, UNIT_TOKENS, PACK], BF16, align_bytes=64, bufs=DEPTH["z_grouped"])
+                z_grouped_of[unit] = z_grouped
+            bank = z_psum.tile([P, 2, GROUP_TOKENS], F32)
+            halves = bank[:].bitcast(BF16).rearrange("p u (c e) -> p u c e", e=2)
+            for out_u, j in ((bank[:, 0, :], 1), (bank[:, 1, :], 3), (halves[:, 0, :, 0], 0), (halves[:, 1, :, 0], 2)):
+                nc.tensor.matmul(out=out_u, lhsT=identity[:], rhs=source[:, j, :], start=True, stop=True)
+            nc.scalar.copy(
+                out=z_grouped_of[unit][:, g * GROUP_TOKENS : (g + 1) * GROUP_TOKENS, :].bitcast(F32),
+                in_=bank[:].rearrange("p u c -> p c u"),
+            )
 
         def quantise(unit, tokens, grouped_of, packed_of, name):
             if unit not in packed_of:
@@ -235,11 +240,11 @@ def tile_blockmlp_mixerblock_pa_t_kernel(tc, y0, W1, b1, W2, b2, out):
 
         def z_stage(unit):
             if unit < UNITS:
-                regroup_z(unit, 0, on_vector if unit < 3 else on_scalar)
-                if unit < 3:
-                    regroup_z(unit, 1, on_vector)
-                else:
-                    regroup_z_through_psum(unit, 1)
+                for g in range(UNIT_GROUPS):
+                    if 3 <= unit < 15:
+                        regroup_z_through_psum(unit, g)
+                    else:
+                        regroup_z(unit, g, on_vector if unit < 3 else on_scalar)
 
         def one_step(step):
             if step + 1 < UNITS:
@@ -266,8 +271,8 @@ def tile_blockmlp_mixerblock_pa_t_kernel(tc, y0, W1, b1, W2, b2, out):
                     layer2_passes(step - 2, i)
             if step < UNITS:
                 for tokens in slices_of(step):
-                    share = 0 if step in (5, 10) or step >= UNITS - 2 else 8
-                    cut = tokens.start + (tokens.stop - tokens.start) * share // 8
+                    share = {UNITS - 2: 8, UNITS - 1: 0}.get(step, 16 if step < 3 else 11)
+                    cut = tokens.start + (tokens.stop - tokens.start) * share // 16
                     if cut > tokens.start:
                         regroup_h(step, slice(tokens.start, cut), on_vector)
                     if cut < tokens.stop:

@@ -25,7 +25,7 @@ PAIRS = GROUPS // UNIT_GROUPS
 RUN = 4
 RUN_H = 8
 DEPTH = {"z_grouped": 4, "z_packed": 3, "h_planes": 3, "h_grouped": 4, "h_packed": 5, "w_grouped": 2}
-PSUM_BANKS = {"hidden": 3, "out": 3, "z": 2}
+PSUM_BANKS = {"hidden": 4, "out": 3, "z": 1}
 FLOPS = 2 * LAYERS * GROUPS * WIDTH * WIDTH * WIDTH
 
 
@@ -223,7 +223,17 @@ def tile_blockmlp_mixerblock_pa_t_kernel(tc, y0, W1, b1, W2, b2, out):
                 in1=b2_raw[:, :, s].unsqueeze(1).to_broadcast([P, GROUP_TOKENS, BLOCKS]),
                 op=ADD,
             )
-            nc.sync.dma_start(out=out_groups[group][:, s * WIDTH : (s + 1) * WIDTH], in_=out_rows[:, s, :])
+            last = s + 1
+            if group == GROUPS - 1 and s >= PACK // 2:
+                first = s
+            elif s % 2:
+                first = s - 1
+            else:
+                return
+            nc.sync.dma_start(
+                out=out_groups[group][:, first * WIDTH : last * WIDTH],
+                in_=out_rows[:, first:last, :].rearrange("p s w -> p (s w)"),
+            )
 
         on_vector = nc.vector.tensor_copy
         on_scalar = nc.scalar.copy
@@ -241,7 +251,7 @@ def tile_blockmlp_mixerblock_pa_t_kernel(tc, y0, W1, b1, W2, b2, out):
         def z_stage(unit):
             if unit < UNITS:
                 for g in range(UNIT_GROUPS):
-                    if 3 <= unit < 15:
+                    if unit >= 3 and g == 1:
                         regroup_z_through_psum(unit, g)
                     else:
                         regroup_z(unit, g, on_vector if unit < 3 else on_scalar)
@@ -271,7 +281,7 @@ def tile_blockmlp_mixerblock_pa_t_kernel(tc, y0, W1, b1, W2, b2, out):
                     layer2_passes(step - 2, i)
             if step < UNITS:
                 for tokens in slices_of(step):
-                    share = {UNITS - 2: 8, UNITS - 1: 0}.get(step, 16 if step < 3 else 11)
+                    share = {UNITS - 2: 8, UNITS - 1: 0}.get(step, 16 if step < 3 else 12 if step < 10 else 10)
                     cut = tokens.start + (tokens.stop - tokens.start) * share // 16
                     if cut > tokens.start:
                         regroup_h(step, slice(tokens.start, cut), on_vector)

@@ -24,6 +24,7 @@ UNITS = GROUPS * BLOCKS // UNIT_GROUPS
 PAIRS = GROUPS // UNIT_GROUPS
 RUN = 4
 RUN_H = 8
+RUN_W = 2
 DEPTH = {"z_grouped": 4, "z_packed": 3, "h_planes": 3, "h_grouped": 4, "h_packed": 5, "w_grouped": 2}
 PSUM_BANKS = {"hidden": 4, "out": 3, "z": 1}
 FLOPS = 2 * LAYERS * GROUPS * WIDTH * WIDTH * WIDTH
@@ -88,8 +89,10 @@ def tile_blockmlp_mixerblock_pa_t_kernel(tc, y0, W1, b1, W2, b2, out):
             first = 0
             for copy, count in shares:
                 copy(
-                    out=w_grouped[:, first : first + count],
-                    in_=w_raw[(layer, block)][:].rearrange("p j (m t) -> p t m j", t=PACK)[:, first : first + count],
+                    out=w_grouped[:, first : first + count].rearrange("p t (m i) j -> p t m j i", i=RUN_W),
+                    in_=w_raw[(layer, block)][:].rearrange("p j (m i t) -> p t m j i", i=RUN_W, t=PACK)[
+                        :, first : first + count
+                    ],
                 )
                 first += count
             nc.vector.quantize_mx(

from contextlib import ExitStack

import concourse.mybir as mybir
from concourse.masks import make_identity

BF16 = mybir.dt.bfloat16
F32 = mybir.dt.float32
U32 = mybir.dt.uint32
U8 = mybir.dt.uint8
FP8X4 = mybir.dt.float8_e4m3fn_x4
GELU = mybir.ActivationFunctionType.Gelu
ADD = mybir.AluOpType.add

P = 128
PACK = 4
WIDTH = P * PACK
BLOCKS = 2
LAYERS = 2
GROUPS = 16
GROUP_TOKENS = WIDTH // BLOCKS
UNIT_GROUPS = 2
UNIT_TOKENS = UNIT_GROUPS * GROUP_TOKENS
UNITS = GROUPS * BLOCKS // UNIT_GROUPS
PAIRS = GROUPS // UNIT_GROUPS
RUN = 4
RUN_H = 8
RUN_W = 2
DEPTH = {"z_grouped": 4, "z_packed": 3, "h_planes": 3, "h_grouped": 4, "h_packed": 5, "w_grouped": 2}
PSUM_BANKS = {"hidden": 4, "out": 3, "z": 1}
FLOPS = 2 * LAYERS * GROUPS * WIDTH * WIDTH * WIDTH


def tile_blockmlp_mixerblock_pa_t_kernel(tc, y0, W1, b1, W2, b2, out):
    nc = tc.nc
    y_groups = y0.rearrange("(g p r) w -> g p (r w)", p=P, r=2)
    out_groups = out.rearrange("(g p r) w -> g p (r w)", p=P, r=2)
    weights = (W1, W2)

    with ExitStack() as stack:
        keep = stack.enter_context(tc.tile_pool(name="keep", bufs=1))
        stage = stack.enter_context(tc.tile_pool(name="stage", bufs=1))
        rows = stack.enter_context(tc.tile_pool(name="rows", bufs=PAIRS + GROUPS // 2))
        hidden_psum = stack.enter_context(tc.psum_pool(name="hidden_psum", bufs=PSUM_BANKS["hidden"]))
        z_psum = stack.enter_context(tc.psum_pool(name="z_psum", bufs=PSUM_BANKS["z"]))
        out_psum = stack.enter_context(tc.psum_pool(name="out_psum", bufs=PSUM_BANKS["out"]))

        w_raw = {}
        y_raw = {}

        def load_weights(layer, block):
            raw = keep.tile([P, PACK, WIDTH], BF16, name="w_raw%d%d" % (layer, block))
            nc.sync.dma_start(out=raw[:], in_=weights[layer][block].rearrange("(p j) h -> p j h", j=PACK))
            w_raw[(layer, block)] = raw

        def load_pair(pair):
            raw = rows.tile([P, UNIT_GROUPS, PACK * WIDTH], BF16, tag="rows", name="y_raw%d" % pair)
            for g in range(UNIT_GROUPS):
                nc.sync.dma_start(out=raw[:, g, :], in_=y_groups[pair * UNIT_GROUPS + g])
            y_raw[pair] = raw

        load_weights(0, 0)
        load_pair(0)
        load_weights(0, 1)
        load_pair(1)
        load_weights(1, 0)
        load_weights(1, 1)
        for pair in range(2, PAIRS):
            load_pair(pair)

        b1_raw = keep.tile([P, BLOCKS, PACK], BF16)
        b2_raw = keep.tile([P, BLOCKS, PACK], BF16)
        nc.scalar.dma_start(out=b1_raw[:], in_=b1.rearrange("n o (m t) -> m (n o) t", t=PACK))
        nc.scalar.dma_start(out=b2_raw[:], in_=b2.rearrange("n o (m t) -> m (n o) t", t=PACK))
        identity = keep.tile([P, P], BF16)
        make_identity(nc, identity[:])

        dummy = keep.tile([P, 1], F32)
        nc.gpsimd.memset(dummy[:], 0.0)
        nc.scalar.activation(out=dummy[:], in_=dummy[:], func=GELU)

        w_words = {}
        w_planes = {}
        for layer in range(LAYERS):
            w_words[layer] = keep.tile([P, BLOCKS, WIDTH], U32, name="w_words%d" % layer, align_bytes=64)
            w_planes[layer] = keep.tile([P, BLOCKS, WIDTH], U8, name="w_planes%d" % layer, align_bytes=64)

        def prepare_weights(layer, block, shares):
            w_grouped = stage.tile([P, PACK, P, PACK], BF16, align_bytes=64, bufs=DEPTH["w_grouped"])
            first = 0
            for copy, count in shares:
                copy(
                    out=w_grouped[:, first : first + count].rearrange("p t (m i) j -> p t m j i", i=RUN_W),
                    in_=w_raw[(layer, block)][:].rearrange("p j (m i t) -> p t m j i", i=RUN_W, t=PACK)[
                        :, first : first + count
                    ],
                )
                first += count
            nc.vector.quantize_mx(
                out=w_words[layer][:, block, :].bitcast(FP8X4),
                scales=w_planes[layer][:, block, :],
                in_=w_grouped[:].rearrange("p t m j -> p (t m j)"),
            )

        z_grouped_of = {}
        z_packed_of = {}
        hidden_banks_of = {}
        h_planes_of = {}
        h_grouped_of = {}
        h_packed_of = {}
        out_banks_of = {}
        out_rows_of = {}

        def slices_of(unit):
            if unit in (0, UNITS - 1):
                return [slice(g * GROUP_TOKENS, (g + 1) * GROUP_TOKENS) for g in range(UNIT_GROUPS)]
            return [slice(0, UNIT_TOKENS)]

        def regroup_z(unit, g, copy):
            pair, block = divmod(unit, BLOCKS)
            if unit not in z_grouped_of:
                z_grouped = stage.tile([P, UNIT_TOKENS, PACK], BF16, align_bytes=64, bufs=DEPTH["z_grouped"])
                z_grouped_of[unit] = z_grouped
            copy(
                out=z_grouped_of[unit][:, g * GROUP_TOKENS : (g + 1) * GROUP_TOKENS, :].rearrange(
                    "p (c i) j -> p c j i", i=RUN
                ),
                in_=y_raw[pair][:, g, :].rearrange("p (j c i n) -> p n c j i", j=PACK, i=RUN, n=BLOCKS)[:, block],
            )

        def regroup_z_through_psum(unit, g):
            pair, block = divmod(unit, BLOCKS)
            source = y_raw[pair][:, g, :].rearrange("p (j c n) -> p n j c", j=PACK, n=BLOCKS)[:, block]
            if unit not in z_grouped_of:
                z_grouped = stage.tile([P, UNIT_TOKENS, PACK], BF16, align_bytes=64, bufs=DEPTH["z_grouped"])
                z_grouped_of[unit] = z_grouped
            bank = z_psum.tile([P, 2, GROUP_TOKENS], F32)
            halves = bank[:].bitcast(BF16).rearrange("p u (c e) -> p u c e", e=2)
            for out_u, j in ((bank[:, 0, :], 1), (bank[:, 1, :], 3), (halves[:, 0, :, 0], 0), (halves[:, 1, :, 0], 2)):
                nc.tensor.matmul(out=out_u, lhsT=identity[:], rhs=source[:, j, :], start=True, stop=True)
            nc.scalar.copy(
                out=z_grouped_of[unit][:, g * GROUP_TOKENS : (g + 1) * GROUP_TOKENS, :].bitcast(F32),
                in_=bank[:].rearrange("p u c -> p c u"),
            )

        def quantise(unit, tokens, grouped_of, packed_of, name):
            if unit not in packed_of:
                words = stage.tile([P, UNIT_TOKENS], U32, align_bytes=64, name=name + "_words", bufs=DEPTH[name])
                plane = stage.tile([P, UNIT_TOKENS], U8, align_bytes=64, name=name + "_plane", bufs=DEPTH[name])
                packed_of[unit] = (words, plane)
            words, plane = packed_of[unit]
            nc.vector.quantize_mx(
                out=words[:, tokens].bitcast(FP8X4),
                scales=plane[:, tokens],
                in_=grouped_of[unit][:, tokens, :].rearrange("p c j -> p (c j)"),
            )

        def quantise_z(unit, tokens):
            quantise(unit, tokens, z_grouped_of, z_packed_of, "z_packed")

        def quantise_h(unit, tokens):
            quantise(unit, tokens, h_grouped_of, h_packed_of, "h_packed")

        def layer1_pass(unit, tokens, t):
            block = unit % BLOCKS
            words, plane = z_packed_of[unit]
            bank = hidden_psum.tile([P, UNIT_TOKENS], F32)
            nc.tensor.matmul_mx(
                out=bank[:, : tokens.stop - tokens.start],
                lhsT=w_words[0][:, block, t * P : (t + 1) * P].bitcast(FP8X4),
                lhsT_scale=w_planes[0][:, block, t * P : (t + 1) * P],
                rhs=words[:, tokens].bitcast(FP8X4),
                rhs_scale=plane[:, tokens],
                start=True,
                stop=True,
            )
            hidden_banks_of[(unit, tokens.start, t)] = bank

        def gelu(unit, tokens):
            block = unit % BLOCKS
            if unit not in h_planes_of:
                h_planes = stage.tile([P, PACK, UNIT_TOKENS], BF16, bufs=DEPTH["h_planes"])
                h_planes_of[unit] = h_planes
            for t in range(PACK):
                nc.scalar.activation(
                    out=h_planes_of[unit][:, t, tokens],
                    in_=hidden_banks_of[(unit, tokens.start, t)][:, : tokens.stop - tokens.start],
                    func=GELU,
                    bias=b1_raw[:, block, t : t + 1],
                    scale=1.0,
                )

        def regroup_h(unit, tokens, copy):
            if unit not in h_grouped_of:
                h_grouped = stage.tile([P, UNIT_TOKENS, PACK], BF16, align_bytes=64, bufs=DEPTH["h_grouped"])
                h_grouped_of[unit] = h_grouped
            copy(
                out=h_grouped_of[unit][:, tokens, :].rearrange("p (c i) t -> p c t i", i=RUN_H),
                in_=h_planes_of[unit][:, :, tokens].rearrange("p t (c i) -> p c t i", i=RUN_H),
            )

        def layer2_passes(group, s):
            pair, half = divmod(group, UNIT_GROUPS)
            tokens = slice(half * GROUP_TOKENS, (half + 1) * GROUP_TOKENS)
            bank = out_psum.tile([P, BLOCKS, GROUP_TOKENS], F32)
            for block in range(BLOCKS):
                words, plane = h_packed_of[pair * BLOCKS + block]
                nc.tensor.matmul_mx(
                    out=bank[:, block, :],
                    lhsT=w_words[1][:, block, s * P : (s + 1) * P].bitcast(FP8X4),
                    lhsT_scale=w_planes[1][:, block, s * P : (s + 1) * P],
                    rhs=words[:, tokens].bitcast(FP8X4),
                    rhs_scale=plane[:, tokens],
                    start=True,
                    stop=True,
                )
            out_banks_of[(group, s)] = bank

        def finish_slice(group, s):
            if group not in out_rows_of:
                out_rows = rows.tile([P, PACK, WIDTH], F32, tag="rows", name="out_rows%d" % group)
                out_rows_of[group] = out_rows
            out_rows = out_rows_of[group]
            nc.vector.tensor_tensor(
                out=out_rows[:, s, :].rearrange("p (c n) -> p c n", n=BLOCKS),
                in0=out_banks_of[(group, s)][:].rearrange("p n c -> p c n"),
                in1=b2_raw[:, :, s].unsqueeze(1).to_broadcast([P, GROUP_TOKENS, BLOCKS]),
                op=ADD,
            )
            last = s + 1
            if group == GROUPS - 1 and s >= PACK // 2:
                first = s
            elif s % 2:
                first = s - 1
            else:
                return
            nc.sync.dma_start(
                out=out_groups[group][:, first * WIDTH : last * WIDTH],
                in_=out_rows[:, first:last, :].rearrange("p s w -> p (s w)"),
            )

        on_vector = nc.vector.tensor_copy
        on_scalar = nc.scalar.copy
        prepare_weights(0, 0, [(on_vector, 4)])
        regroup_z(0, 0, on_scalar)
        regroup_z(0, 1, on_vector)
        for tokens in slices_of(0):
            quantise_z(0, tokens)
            for t in range(PACK):
                layer1_pass(0, tokens, t)
        regroup_z(1, 0, on_vector)
        regroup_z(1, 1, on_scalar)
        prepare_weights(0, 1, [(on_vector, 4)])

        def z_stage(unit):
            if unit < UNITS:
                for g in range(UNIT_GROUPS):
                    if unit >= 3 and g == 1:
                        regroup_z_through_psum(unit, g)
                    else:
                        regroup_z(unit, g, on_vector if unit < 3 else on_scalar)

        def one_step(step):
            if step + 1 < UNITS:
                for tokens in slices_of(step + 1):
                    quantise_z(step + 1, tokens)
            if step in (1, 2):
                prepare_weights(1, step - 1, [(on_vector, 4)])
            if 0 <= step - 1 < UNITS:
                for tokens in slices_of(step - 1):
                    quantise_h(step - 1, tokens)
            if 0 <= step - 3 < GROUPS:
                for s in range(PACK):
                    finish_slice(step - 3, s)
            if step < UNITS:
                for tokens in slices_of(step):
                    gelu(step, tokens)
            for tokens in slices_of(step + 1) if step + 1 == UNITS - 1 else []:
                for t in range(PACK):
                    layer1_pass(step + 1, tokens, t)
            for i in range(PACK):
                if step + 1 < UNITS - 1:
                    layer1_pass(step + 1, slice(0, UNIT_TOKENS), i)
                if 0 <= step - 2 < GROUPS:
                    layer2_passes(step - 2, i)
            if step < UNITS:
                for tokens in slices_of(step):
                    share = {UNITS - 2: 8, UNITS - 1: 0}.get(step, 16 if step < 3 else 12 if step < 10 else 10)
                    cut = tokens.start + (tokens.stop - tokens.start) * share // 16
                    if cut > tokens.start:
                        regroup_h(step, slice(tokens.start, cut), on_vector)
                    if cut < tokens.stop:
                        regroup_h(step, slice(cut, tokens.stop), on_scalar)
            z_stage(step + 2)

        for step in range(UNITS + 3):
            one_step(step)
